import numpy as np
import ml_dtypes


def mxq(x, axis, fmt="e4m3"):
    dtype, down = {"e4m3": (ml_dtypes.float8_e4m3fn, 7), "e5m2": (ml_dtypes.float8_e5m2, 14)}[fmt]
    v = np.moveaxis(np.asarray(x, np.float32).astype(ml_dtypes.bfloat16).astype(np.float64), axis, -1)
    blocks = v.reshape(v.shape[:-1] + (-1, 32))
    amax = np.abs(blocks).max(-1, keepdims=True)
    byte = np.maximum(np.where(amax > 0, np.frexp(amax)[1] - 1 + 127, 0) - down, 1)
    scale = np.exp2(byte - 127.0)
    codes = (blocks / scale).astype(np.float32).astype(dtype).astype(np.float64)
    return np.moveaxis((codes * scale).reshape(v.shape), -1, axis)


WIDE = False


def mx_kscale(k):
    if not WIDE:
        return np.ones(k)
    levels = np.array([18, -18])
    if k % 512:
        return np.exp2(np.random.permutation(np.resize(levels, k // 32))).repeat(32)
    a = np.empty((k // 512, 16))
    for p in range(k // 512):
        a[p, :8] = np.random.permutation(np.resize(levels, 8))
        for g in range(8):
            far = levels[np.abs(levels - a[p, g]) >= 10]
            a[p, g + 8] = far[np.random.randint(len(far))]
    return np.exp2(a.ravel()).repeat(32)


BF16 = ml_dtypes.bfloat16


def bf(x):
    return np.asarray(x, np.float32).astype(BF16)


def f64(x):
    return np.asarray(x).astype(np.float64)


B, C, H, W, R = 2, 512, 64, 32, 4
N = H * W
EPS = 1e-12
NOISE = 0.5
GS = 256.0


def mix(a, z):
    return sum(a[:, :, r, None] * z[:, r, None, :] for r in range(R))


def rnorm(x):
    n = np.sqrt((x * x).sum(2))
    return 1.0 / np.maximum(n, EPS)


def setup_inputs():
    v = mx_kscale(C)
    z = np.random.standard_normal((B, R, N))
    a1 = np.random.standard_normal((B, C, R)) / np.sqrt(R)
    a2 = np.random.standard_normal((B, C, R)) / np.sqrt(R)
    x10 = bf(mix(a1, z) + NOISE * np.random.standard_normal((B, C, N)))
    x20 = bf(mix(a2, z) + NOISE * np.random.standard_normal((B, C, N)))
    r1 = rnorm(f64(x10))
    r2 = rnorm(f64(x20))
    x1 = bf((f64(x10) / v[None, :, None]).reshape(B, C, H, W))
    x2 = bf((f64(x20) / v[None, :, None]).reshape(B, C, H, W))
    vv = v[None, :, None] * v[None, None, :] * GS
    g0 = bf(np.random.standard_normal((B, C, C)) * np.exp2(np.random.randint(-6, 1, (B, C, 1))) * vv)
    g1 = bf(np.random.standard_normal((B, C, C)) * np.exp2(np.random.randint(-6, 1, (B, C, 1))) * vv)
    return {"x1": x1, "x2": x2, "r1": np.asarray(r1, np.float32), "r2": np.asarray(r2, np.float32),
            "grad_0": g0, "grad_1": g1}


def reference(x1, x2, r1, r2, grad_0, grad_1):
    ra = f64(r1)[:, :, None]
    rb = f64(r2)[:, :, None]
    u1 = f64(x1).reshape(B, C, N) * ra
    u2 = f64(x2).reshape(B, C, N) * rb
    g0 = f64(grad_0)
    g1 = f64(grad_1)
    g0t = g0.transpose(0, 2, 1)
    g1t = g1.transpose(0, 2, 1)
    d1 = np.concatenate([g0 + g0t, g1 + g0t], axis=2)
    d2 = np.concatenate([g0 + g1t, g1 + g1t], axis=2)
    uq = mxq(np.concatenate([u1, u2], axis=1), 1, "e4m3")
    du1 = mxq(d1, 2, "e5m2") @ uq
    du2 = mxq(d2, 2, "e5m2") @ uq
    s1 = (u1 * du1).sum(2, keepdims=True)
    s2 = (u2 * du2).sum(2, keepdims=True)
    dx1 = ra * (du1 - u1 * s1)
    dx2 = rb * (du2 - u2 * s2)
    return dx1.reshape(B, C, H, W), dx2.reshape(B, C, H, W)

@@ -1,0 +1,316 @@
+from contextlib import ExitStack
+
+import concourse.mybir as mybir
+from concourse.masks import make_identity
+
+F32 = mybir.dt.float32
+BF16 = mybir.dt.bfloat16
+U32 = mybir.dt.uint32
+U8 = mybir.dt.uint8
+E4X4 = mybir.dt.float8_e4m3fn_x4
+E5X4 = mybir.dt.float8_e5m2_x4
+ALU = mybir.AluOpType
+COPY = mybir.ActivationFunctionType.Copy
+
+NB, C, N = 2, 512, 2048
+P = 128
+J = 4
+NT = 512
+NCH = N // NT
+FLOPS = 2 * 2 * NB * C * (2 * C) * N
+
+V_INTERLEAVE = (0, 2, 4, 6)
+GN = 128
+G_BANKS = {8: (2,), 9: (2,), 10: (2,), 11: (2,), 12: (2,), 13: (2, 3), 14: (3,), 15: (2, 3)}
+S_BLOCKS = ()
+S_AT = {0: 0, 1: 1, 2: 2, 3: 2, 4: 3, 5: 4, 6: 5, 7: 6}
+
+
+def tile_interfusion_pa_v_kernel(tc, x1, x2, r1, r2, grad_0, grad_1, out_0, out_1):
+    nc = tc.nc
+    x_hbm = [x.rearrange("b (p j) h w -> b p j (h w)", j=J) for x in (x1, x2)]
+    g_hbm = [g.rearrange("b (p j) w -> b p j w", j=J) for g in (grad_0, grad_1)]
+    o_hbm = [o.rearrange("b (p j) h w -> b p j (h w)", j=J) for o in (out_0, out_1)]
+
+    with ExitStack() as ctx:
+        keep = ctx.enter_context(tc.tile_pool(name="keep", bufs=1))
+        stage = ctx.enter_context(tc.tile_pool(name="stage", bufs=3))
+        psum_du = ctx.enter_context(tc.psum_pool(name="psum_du", bufs=6))
+        psum_d = ctx.enter_context(tc.psum_pool(name="psum_d", bufs=2))
+
+        ident = keep.tile([P, P], BF16, name="ident", align_bytes=64)
+        make_identity(nc, ident[:])
+        r_sb = keep.tile([P, 2, NB, J], F32, name="r_sb")
+        nr2 = keep.tile([P, 2, NB, J], F32, name="nr2")
+        x_sb = [[keep.tile([P, J, N], BF16, name="x_%d_%d" % (b, i), align_bytes=64) for i in range(2)] for b in range(NB)]
+        g_sb = [[keep.tile([P, J, C], BF16, name="g_%d_%d" % (b, i), align_bytes=64) for i in range(2)] for b in range(NB)]
+        u_codes = [keep.tile([P, 2, N], U32, name="uc_%d" % b, align_bytes=64) for b in range(NB)]
+        u_scales = [keep.tile([P, 2, N], U8, name="us_%d" % b, align_bytes=64) for b in range(NB)]
+
+        scaled = {}
+        grouped = {}
+        d_banks = {}
+        d_grouped = {}
+        d_codes = {}
+        d_scales = {}
+        du = {}
+        q4 = {}
+        coef = {}
+        t_sb = {}
+        rdu = {}
+        o_sb = {}
+
+        def where(i):
+            return i // 8, i % 4, 1 if i % 8 < 4 else 0
+
+        def u_scale(b, k):
+            n, xi = k // 2, k % 2
+            s = stage.tile([P, J, NT], BF16, name="scaled", bufs=3, align_bytes=64)
+            for j in range(J):
+                nc.vector.tensor_scalar(out=s[:, j, :], in0=x_sb[b][xi][:, j, n * NT : (n + 1) * NT],
+                                        scalar1=r_sb[:, xi, b, j : j + 1], scalar2=None, op0=ALU.mult)
+            scaled[b, k] = s
+
+        def u_interleave(b, k, on_vector):
+            g = stage.tile([P, NT, J], BF16, name="grouped", bufs=3, align_bytes=64)
+            src = scaled.pop((b, k))[:].rearrange("p j n -> p n j")
+            if on_vector:
+                nc.vector.tensor_copy(out=g[:], in_=src)
+            else:
+                nc.scalar.copy(out=g[:], in_=src)
+            grouped[b, k] = g
+
+        def u_scale_interleave(b, k):
+            n, xi = k // 2, k % 2
+            g = stage.tile([P, NT, J], BF16, name="grouped1", bufs=4, align_bytes=64)
+            for c in range(0, NT, GN):
+                nc.gpsimd.tensor_tensor(out=g[:, c : c + GN, :], in0=x_sb[b][xi][:, :, n * NT + c : n * NT + c + GN].rearrange("p j n -> p n j"),
+                                        in1=r_sb[:, xi, b, :].unsqueeze(1).to_broadcast([P, GN, J]), op=ALU.mult)
+            grouped[b, k] = g
+
+        def u_scale_g(b, k):
+            n, xi = k // 2, k % 2
+            s = stage.tile([P, J, NT], BF16, name="scaled", bufs=3, align_bytes=64)
+            for j in range(J):
+                nc.gpsimd.tensor_scalar(out=s[:, j, :], in0=x_sb[b][xi][:, j, n * NT : (n + 1) * NT],
+                                        scalar1=r_sb[:, xi, b, j : j + 1], scalar2=0.0, op0=ALU.mult, op1=ALU.add)
+            scaled[b, k] = s
+
+        def u_interleave_s(b, k):
+            g = stage.tile([P, NT, J], BF16, name="grouped1", bufs=4, align_bytes=64)
+            s = scaled.pop((b, k))
+            for c in range(0, NT, GN):
+                nc.scalar.copy(out=g[:, c : c + GN, :], in_=s[:, :, c : c + GN].rearrange("p j n -> p n j"))
+            grouped[b, k] = g
+
+        def u_quantize(b, k):
+            n, xi = k // 2, k % 2
+            cols = slice(n * NT, (n + 1) * NT)
+            nc.vector.quantize_mx(out=u_codes[b][:, xi, cols].bitcast(E4X4), scales=u_scales[b][:, xi, cols],
+                                  in_=grouped.pop((b, k))[:].rearrange("p n j -> p (n j)"))
+
+        def d_prepare(i):
+            b, tt, o = where(i)
+            banks = []
+            for ps in range(2):
+                if o == 0 and ps == 1:
+                    bank = psum_d.tile([P, J, P], BF16, name="dbank")
+                    for t in range(J):
+                        nc.tensor.transpose(bank[:, t, :], d_grouped[8 * b + t][:, 0, :, tt], ident[:])
+                else:
+                    bank = psum_d.tile([P, J, P], F32, name="dbank")
+                    for t in range(J):
+                        nc.tensor.matmul(bank[:, t, :], lhsT=ident[:], rhs=g_sb[b][o][:, t, tt::J], start=True, stop=False)
+                        nc.tensor.matmul(bank[:, t, :], lhsT=g_sb[b][ps][:, tt, t::J], rhs=ident[:], start=False, stop=True)
+                banks.append(bank)
+            d_banks[i] = banks
+
+        def d_round(i):
+            if where(i)[2] == 1:
+                dg = stage.tile([P, 2, P, J], BF16, name="dg1", bufs=4, align_bytes=64)
+            else:
+                dg = stage.tile([P, 2, P, J], BF16, name="dg0", bufs=3, align_bytes=64)
+            for ps in range(2):
+                nc.scalar.copy(out=dg[:, ps, :, :], in_=d_banks[i][ps][:].rearrange("p t m -> p m t"))
+            d_grouped[i] = dg
+
+        def d_quantize(i):
+            dc = stage.tile([P, 2 * P], U32, name="dc", bufs=6, align_bytes=64)
+            dsc = stage.tile([P, 2 * P], U8, name="dsc", bufs=6, align_bytes=64)
+            nc.vector.quantize_mx(out=dc[:].bitcast(E5X4), scales=dsc[:], in_=d_grouped[i][:].rearrange("p s m t -> p (s m t)"))
+            d_codes[i], d_scales[i] = dc, dsc
+
+        def fill(m):
+            i, n = m // NCH, m % NCH
+            b = where(i)[0]
+            if m < 62:
+                bank = psum_du.tile([P, NT], F32, name="du")
+            else:
+                bank = psum_d.tile([P, NT], F32, name="dbank")
+            cols = slice(n * NT, (n + 1) * NT)
+            for ps in range(2):
+                ks = slice(ps * P, (ps + 1) * P)
+                nc.tensor.matmul_mx(out=bank[:], lhsT=d_codes[i][:, ks].bitcast(E5X4), lhsT_scale=d_scales[i][:, ks],
+                                    rhs=u_codes[b][:, ps, cols].bitcast(E4X4), rhs_scale=u_scales[b][:, ps, cols],
+                                    start=(ps == 0), stop=(ps == 1))
+            du[i, n] = bank
+
+        def row_sum(i, n):
+            b, tt, o = where(i)
+            if n == 0:
+                q = stage.tile([P, NCH], F32, name="q4", bufs=3)
+                q4[i] = q
+            junk = stage.tile([P, NT], BF16, name="junk", bufs=4)
+            nc.vector.scalar_tensor_tensor(out=junk[:], in0=du[i, n][:], scalar=r_sb[:, o, b, tt : tt + 1],
+                                           in1=x_sb[b][o][:, tt, n * NT : (n + 1) * NT], op0=ALU.mult, op1=ALU.mult,
+                                           accum_out=q4[i][:, n : n + 1])
+
+        def coefficient(i):
+            b, tt, o = where(i)
+            cf = stage.tile([P, 1], F32, name="cf", bufs=3)
+            junk4 = stage.tile([P, NCH], F32, name="junk4", bufs=3)
+            nc.scalar.activation(out=junk4[:], in_=q4[i][:], func=COPY, scale=nr2[:, o, b, tt : tt + 1], accum_out=cf[:])
+            coef[i] = cf
+            t = stage.tile([P, N], F32, name="t", bufs=2)
+            ob = stage.tile([P, N], F32, name="o", bufs=3)
+            t_sb[i], o_sb[i] = t, ob
+
+        def projection(i, n):
+            b, tt, o = where(i)
+            cols = slice(n * NT, (n + 1) * NT)
+            nc.scalar.activation(out=t_sb[i][:, cols], in_=x_sb[b][o][:, tt, cols], func=COPY, scale=coef[i][:])
+
+        def scaled_du(i, n):
+            b, tt, o = where(i)
+            rd = stage.tile([P, NT], F32, name="rdu", bufs=4)
+            nc.scalar.activation(out=rd[:], in_=du[i, n][:], func=COPY, scale=r_sb[:, o, b, tt : tt + 1])
+            rdu[i, n] = rd
+
+        def finish(i, n):
+            b, tt, o = where(i)
+            last = i == 15
+            cols = slice(n * NT, (n + 1) * NT)
+            if last and (i, n) in rdu:
+                nc.vector.scalar_tensor_tensor(out=o_sb[i][:, cols], in0=x_sb[b][o][:, tt, cols], scalar=coef[i][:],
+                                               in1=rdu.pop((i, n))[:], op0=ALU.mult, op1=ALU.add)
+            elif (i, n) in rdu:
+                nc.gpsimd.tensor_tensor(out=o_sb[i][:, cols], in0=rdu.pop((i, n))[:], in1=t_sb[i][:, cols], op=ALU.add)
+            else:
+                nc.vector.scalar_tensor_tensor(out=o_sb[i][:, cols], in0=du[i, n][:], scalar=r_sb[:, o, b, tt : tt + 1],
+                                               in1=t_sb[i][:, cols], op0=ALU.mult, op1=ALU.add)
+
+        def store(i, n0, n1):
+            b, tt, o = where(i)
+            nc.sync.dma_start(out=o_hbm[o][b, :, tt, n0:n1], in_=o_sb[i][:, n0:n1])
+
+        with tc.manual_schedule():
+            for xi, r in enumerate((r1, r2)):
+                nc.scalar.dma_start(out=r_sb[:, xi, :, :], in_=r.rearrange("b (p j) -> p b j", j=J))
+
+            def load_x(b, n0, n1):
+                for xi in range(2):
+                    nc.sync.dma_start(out=x_sb[b][xi][:, :, n0:n1], in_=x_hbm[xi][b, :, :, n0:n1])
+
+            def load_g(b):
+                for gi in range(2):
+                    nc.sync.dma_start(out=g_sb[b][gi][:], in_=g_hbm[gi][b])
+
+            load_x(0, 0, 512)
+            load_x(0, 512, 1024)
+            load_g(0)
+            load_x(0, 1024, 2048)
+            load_x(1, 0, 1024)
+            load_x(1, 1024, 2048)
+            load_g(1)
+
+            warm = keep.tile([P, 1], F32, name="warm")
+            nc.vector.memset(warm[:], 0.0)
+            nc.scalar.activation(out=warm[:], in_=warm[:], func=COPY)
+            nc.vector.scalar_tensor_tensor(out=nr2[:].rearrange("p i b j -> p (i b j)"), in0=r_sb[:].rearrange("p i b j -> p (i b j)"),
+                                           scalar=-1.0, in1=r_sb[:].rearrange("p i b j -> p (i b j)"), op0=ALU.mult, op1=ALU.mult)
+
+            for s in range(10):
+                if s < 8:
+                    u_scale(0, s)
+                if 1 <= s <= 8:
+                    u_interleave(0, s - 1, (s - 1) in V_INTERLEAVE)
+                if s in (4, 5, 6):
+                    d_prepare(s - 4)
+                    d_round(s - 4)
+                if s == 6:
+                    d_quantize(0)
+                if s == 8:
+                    d_quantize(1)
+                    for m in range(3):
+                        fill(m)
+                if s == 9:
+                    row_sum(0, 0)
+                    row_sum(0, 1)
+                if s >= 2:
+                    u_quantize(0, s - 2)
+            fill(3)
+            fill(4)
+            fill(5)
+            d_prepare(3)
+            def g_block(k):
+                if k in S_BLOCKS:
+                    u_scale_g(1, k)
+                else:
+                    u_scale_interleave(1, k)
+
+            for k in range(2):
+                g_block(k)
+
+            quant_at = {1: (0,), 2: (1,), 3: (2, 3), 4: (4,), 5: (5,), 6: (6,), 7: (7,)}
+            n_g = 2
+            for i in range(16):
+                g_banks = G_BANKS.get(i, ())
+                if i < 15:
+                    row_sum(i, 2)
+                    row_sum(i, 3)
+                    if 2 in g_banks:
+                        scaled_du(i, 2)
+                    coefficient(i)
+                    projection(i, 0)
+                    projection(i, 1)
+                    if 3 in g_banks:
+                        scaled_du(i, 3)
+                    for n in (2, 3) if 2 not in g_banks or 3 in g_banks else (3, 2):
+                        projection(i, n)
+                else:
+                    for n in g_banks:
+                        scaled_du(i, n)
+                    coefficient(i)
+                    projection(i, 0)
+                    projection(i, 1)
+                if i + 3 < 16:
+                    d_round(i + 3)
+                for k in S_BLOCKS:
+                    if i == max(0, S_AT[k]):
+                        u_interleave_s(1, k)
+                for k in quant_at.get(i, ()):
+                    u_quantize(1, k)
+                while n_g < 8 and n_g <= i + 3:
+                    g_block(n_g)
+                    n_g += 1
+                if i + 1 < 16:
+                    row_sum(i + 1, 0)
+                    row_sum(i + 1, 1)
+                if i + 2 < 16:
+                    d_quantize(i + 2)
+                if i == 14:
+                    row_sum(15, 2)
+                    row_sum(15, 3)
+                for n in (2, 3, 0, 1) if i == 15 else range(NCH):
+                    finish(i, n)
+                    if 4 * i + 6 + n < 62:
+                        fill(4 * i + 6 + n)
+                    if i == 15:
+                        store(i, n * NT, (n + 1) * NT)
+                    elif n % 2 == 1:
+                        store(i, (n - 1) * NT, (n + 1) * NT)
+                if i == 13:
+                    fill(62)
+                    fill(63)
+                if i + 4 < 16:
+                    d_prepare(i + 4)

@@ -41,6 +41,7 @@ def tile_interfusion_pa_v_kernel(tc, x1, x2, r1, r2, grad_0, grad_1, out_0, out_
         ident = keep.tile([P, P], BF16, name="ident", align_bytes=64)
         make_identity(nc, ident[:])
         r_sb = keep.tile([P, 2, NB, J], F32, name="r_sb")
+        r_late = keep.tile([P, 2, J], F32, name="r_late")
         nr2 = keep.tile([P, 2, NB, J], F32, name="nr2")
         x_sb = [[keep.tile([P, J, N], BF16, name="x_%d_%d" % (b, i), align_bytes=64) for i in range(2)] for b in range(NB)]
         g_sb = [[keep.tile([P, J, C], BF16, name="g_%d_%d" % (b, i), align_bytes=64) for i in range(2)] for b in range(NB)]
@@ -73,19 +74,20 @@ def tile_interfusion_pa_v_kernel(tc, x1, x2, r1, r2, grad_0, grad_1, out_0, out_
 
         def u_interleave(b, k, on_vector):
             g = stage.tile([P, NT, J], BF16, name="grouped", bufs=3, align_bytes=64)
-            src = scaled.pop((b, k))[:].rearrange("p j n -> p n j")
+            src = scaled.pop((b, k))[:].rearrange("p j (c i) -> p c j i", i=4)
+            dst = g[:].rearrange("p (c i) j -> p c j i", i=4)
             if on_vector:
-                nc.vector.tensor_copy(out=g[:], in_=src)
+                nc.vector.tensor_copy(out=dst, in_=src)
             else:
-                nc.scalar.copy(out=g[:], in_=src)
+                nc.scalar.copy(out=dst, in_=src)
             grouped[b, k] = g
 
         def u_scale_interleave(b, k):
             n, xi = k // 2, k % 2
-            g = stage.tile([P, NT, J], BF16, name="grouped1", bufs=4, align_bytes=64)
+            g = stage.tile([P, NT, J], BF16, name="grouped1", bufs=2, align_bytes=64)
             for c in range(0, NT, GN):
                 nc.gpsimd.tensor_tensor(out=g[:, c : c + GN, :], in0=x_sb[b][xi][:, :, n * NT + c : n * NT + c + GN].rearrange("p j n -> p n j"),
-                                        in1=r_sb[:, xi, b, :].unsqueeze(1).to_broadcast([P, GN, J]), op=ALU.mult)
+                                        in1=r_late[:, xi, :].unsqueeze(1).to_broadcast([P, GN, J]), op=ALU.mult)
             grouped[b, k] = g
 
         def u_scale_g(b, k):
@@ -248,6 +250,7 @@ def tile_interfusion_pa_v_kernel(tc, x1, x2, r1, r2, grad_0, grad_1, out_0, out_
                     row_sum(0, 1)
                 if s >= 2:
                     u_quantize(0, s - 2)
+            nc.vector.tensor_copy(out=r_late[:], in_=r_sb[:, :, 1, :])
             fill(3)
             fill(4)
             fill(5)
@@ -261,8 +264,7 @@ def tile_interfusion_pa_v_kernel(tc, x1, x2, r1, r2, grad_0, grad_1, out_0, out_
             for k in range(2):
                 g_block(k)
 
-            quant_at = {1: (0,), 2: (1,), 3: (2, 3), 4: (4,), 5: (5,), 6: (6,), 7: (7,)}
-            n_g = 2
+            quant_at = {1: (0,), 2: (1,), 3: (2,), 4: (3,), 5: (4,), 6: (5,), 7: (6, 7)}
             for i in range(16):
                 g_banks = G_BANKS.get(i, ())
                 if i < 15:
@@ -288,15 +290,16 @@ def tile_interfusion_pa_v_kernel(tc, x1, x2, r1, r2, grad_0, grad_1, out_0, out_
                 for k in S_BLOCKS:
                     if i == max(0, S_AT[k]):
                         u_interleave_s(1, k)
+                if i + 2 < 16 and i < 8:
+                    d_quantize(i + 2)
                 for k in quant_at.get(i, ()):
                     u_quantize(1, k)
-                while n_g < 8 and n_g <= i + 3:
-                    g_block(n_g)
-                    n_g += 1
+                    if k + 2 < 8:
+                        g_block(k + 2)
                 if i + 1 < 16:
                     row_sum(i + 1, 0)
                     row_sum(i + 1, 1)
-                if i + 2 < 16:
+                if i + 2 < 16 and i >= 8:
                     d_quantize(i + 2)
                 if i == 14:
                     row_sum(15, 2)

@@ -21,9 +21,21 @@ FLOPS = 2 * 2 * NB * C * (2 * C) * N
 
 V_INTERLEAVE = (0, 2, 4, 6)
 GN = 128
-G_BANKS = {8: (2,), 9: (2,), 10: (2,), 11: (2,), 12: (2,), 13: (2, 3), 14: (3,), 15: (2, 3)}
-S_BLOCKS = ()
-S_AT = {0: 0, 1: 1, 2: 2, 3: 2, 4: 3, 5: 4, 6: 5, 7: 6}
+G_BANKS = {8: (2, 3), 9: (2, 3), 10: (2, 3), 11: (2, 3), 12: (2, 3), 13: (3,), 14: (2, 3), 15: (2, 3), 1: (3,), 6: (3,), 7: (1, 2, 3), 3: (), 5: (), 2: (3,), 0: (), 4: ()}
+R_ENG = {0: 'G', 1: 'S', 2: 'S', 3: 'S', 4: 'G', 5: 'S', 6: 'S', 7: 'G', 14: 'S', 9: 'G', 12: 'S', 8: 'G', 11: 'G', 10: 'S', 13: 'G'}
+QD_EARLY = (0, 2, 3, 5, 6)
+OB = 3
+G1BUFS = 6
+S_SCALE = (3,)
+D_AT = {6: 0, 8: 1, 9: 2}
+DQ_AT = {8: 0, 9: 1}
+A_AT = 8
+STORE_LAST = 0
+S_PIECES = 1
+S_BLOCKS = (1, 2, 3, 4, 5, 6, 7)
+S_AT = {2: (0, 1), 4: (2, 3), 5: (4,), 6: (5, 6, 7)}
+QUANT_AT = {2: (0,), 5: (1,), 6: (2, 3), 7: (4, 5, 6, 7)}
+G_AT = {0: (0, 1, 2, 3), 4: (4,), 5: (5, 6, 7)}
 
 
 def tile_interfusion_pa_v_kernel(tc, x1, x2, r1, r2, grad_0, grad_1, out_0, out_1):
@@ -42,6 +54,7 @@ def tile_interfusion_pa_v_kernel(tc, x1, x2, r1, r2, grad_0, grad_1, out_0, out_
         make_identity(nc, ident[:])
         r_sb = keep.tile([P, 2, NB, J], F32, name="r_sb")
         r_late = keep.tile([P, 2, J], F32, name="r_late")
+        nr1 = keep.tile([P, 2, NB, J], F32, name="nr1")
         nr2 = keep.tile([P, 2, NB, J], F32, name="nr2")
         x_sb = [[keep.tile([P, J, N], BF16, name="x_%d_%d" % (b, i), align_bytes=64) for i in range(2)] for b in range(NB)]
         g_sb = [[keep.tile([P, J, C], BF16, name="g_%d_%d" % (b, i), align_bytes=64) for i in range(2)] for b in range(NB)]
@@ -68,8 +81,12 @@ def tile_interfusion_pa_v_kernel(tc, x1, x2, r1, r2, grad_0, grad_1, out_0, out_
             n, xi = k // 2, k % 2
             s = stage.tile([P, J, NT], BF16, name="scaled", bufs=3, align_bytes=64)
             for j in range(J):
-                nc.vector.tensor_scalar(out=s[:, j, :], in0=x_sb[b][xi][:, j, n * NT : (n + 1) * NT],
-                                        scalar1=r_sb[:, xi, b, j : j + 1], scalar2=None, op0=ALU.mult)
+                src = x_sb[b][xi][:, j, n * NT : (n + 1) * NT]
+                r = r_sb[:, xi, b, j : j + 1]
+                if k in S_SCALE:
+                    nc.scalar.activation(out=s[:, j, :], in_=src, func=COPY, scale=r)
+                else:
+                    nc.vector.tensor_scalar(out=s[:, j, :], in0=src, scalar1=r, scalar2=None, op0=ALU.mult)
             scaled[b, k] = s
 
         def u_interleave(b, k, on_vector):
@@ -84,7 +101,7 @@ def tile_interfusion_pa_v_kernel(tc, x1, x2, r1, r2, grad_0, grad_1, out_0, out_
 
         def u_scale_interleave(b, k):
             n, xi = k // 2, k % 2
-            g = stage.tile([P, NT, J], BF16, name="grouped1", bufs=2, align_bytes=64)
+            g = stage.tile([P, NT, J], BF16, name="grouped1", bufs=G1BUFS, align_bytes=64)
             for c in range(0, NT, GN):
                 nc.gpsimd.tensor_tensor(out=g[:, c : c + GN, :], in0=x_sb[b][xi][:, :, n * NT + c : n * NT + c + GN].rearrange("p j n -> p n j"),
                                         in1=r_late[:, xi, :].unsqueeze(1).to_broadcast([P, GN, J]), op=ALU.mult)
@@ -92,17 +109,18 @@ def tile_interfusion_pa_v_kernel(tc, x1, x2, r1, r2, grad_0, grad_1, out_0, out_
 
         def u_scale_g(b, k):
             n, xi = k // 2, k % 2
-            s = stage.tile([P, J, NT], BF16, name="scaled", bufs=3, align_bytes=64)
+            s = stage.tile([P, 2, NT, 2], BF16, name="scaled", bufs=3, align_bytes=64)
             for j in range(J):
-                nc.gpsimd.tensor_scalar(out=s[:, j, :], in0=x_sb[b][xi][:, j, n * NT : (n + 1) * NT],
-                                        scalar1=r_sb[:, xi, b, j : j + 1], scalar2=0.0, op0=ALU.mult, op1=ALU.add)
+                nc.gpsimd.tensor_scalar(out=s[:, j // 2, :, j % 2], in0=x_sb[b][xi][:, j, n * NT : (n + 1) * NT],
+                                        scalar1=r_late[:, xi, j : j + 1], scalar2=0.0, op0=ALU.mult, op1=ALU.add)
             scaled[b, k] = s
 
         def u_interleave_s(b, k):
-            g = stage.tile([P, NT, J], BF16, name="grouped1", bufs=4, align_bytes=64)
-            s = scaled.pop((b, k))
-            for c in range(0, NT, GN):
-                nc.scalar.copy(out=g[:, c : c + GN, :], in_=s[:, :, c : c + GN].rearrange("p j n -> p n j"))
+            g = stage.tile([P, NT, J], BF16, name="grouped1", bufs=G1BUFS, align_bytes=64)
+            s = scaled.pop((b, k))[:].rearrange("p u n e -> p u (n e)").bitcast(F32)
+            d = g[:].bitcast(F32)
+            for c in range(0, NT, NT // S_PIECES):
+                nc.scalar.copy(out=d[:, c : c + NT // S_PIECES, :], in_=s[:, :, c : c + NT // S_PIECES].rearrange("p u n -> p n u"))
             grouped[b, k] = g
 
         def u_quantize(b, k):
@@ -167,20 +185,22 @@ def tile_interfusion_pa_v_kernel(tc, x1, x2, r1, r2, grad_0, grad_1, out_0, out_
                                            in1=x_sb[b][o][:, tt, n * NT : (n + 1) * NT], op0=ALU.mult, op1=ALU.mult,
                                            accum_out=q4[i][:, n : n + 1])
 
-        def coefficient(i):
+        def coefficient(i, both):
             b, tt, o = where(i)
-            cf = stage.tile([P, 1], F32, name="cf", bufs=3)
-            junk4 = stage.tile([P, NCH], F32, name="junk4", bufs=3)
-            nc.scalar.activation(out=junk4[:], in_=q4[i][:], func=COPY, scale=nr2[:, o, b, tt : tt + 1], accum_out=cf[:])
+            cf = stage.tile([P, 2], F32, name="cf", bufs=3)
+            junk4 = stage.tile([P, 2, NCH], F32, name="junk4", bufs=3)
+            for v in range(2 if both else 1):
+                nc.scalar.activation(out=junk4[:, v, :], in_=q4[i][:], func=COPY, scale=(nr1, nr2)[v][:, o, b, tt : tt + 1],
+                                     accum_out=cf[:, v : v + 1])
             coef[i] = cf
-            t = stage.tile([P, N], F32, name="t", bufs=2)
-            ob = stage.tile([P, N], F32, name="o", bufs=3)
-            t_sb[i], o_sb[i] = t, ob
+            ob = stage.tile([P, N], F32, name="o", bufs=OB)
+            o_sb[i] = ob
 
         def projection(i, n):
             b, tt, o = where(i)
-            cols = slice(n * NT, (n + 1) * NT)
-            nc.scalar.activation(out=t_sb[i][:, cols], in_=x_sb[b][o][:, tt, cols], func=COPY, scale=coef[i][:])
+            t = stage.tile([P, NT], F32, name="t", bufs=4)
+            nc.scalar.activation(out=t[:], in_=x_sb[b][o][:, tt, n * NT : (n + 1) * NT], func=COPY, scale=coef[i][:, 1:2])
+            t_sb[i, n] = t
 
         def scaled_du(i, n):
             b, tt, o = where(i)
@@ -188,18 +208,26 @@ def tile_interfusion_pa_v_kernel(tc, x1, x2, r1, r2, grad_0, grad_1, out_0, out_
             nc.scalar.activation(out=rd[:], in_=du[i, n][:], func=COPY, scale=r_sb[:, o, b, tt : tt + 1])
             rdu[i, n] = rd
 
-        def finish(i, n):
+        def project(i, n):
             b, tt, o = where(i)
-            last = i == 15
             cols = slice(n * NT, (n + 1) * NT)
-            if last and (i, n) in rdu:
-                nc.vector.scalar_tensor_tensor(out=o_sb[i][:, cols], in0=x_sb[b][o][:, tt, cols], scalar=coef[i][:],
+            if (i, n) in rdu:
+                nc.vector.scalar_tensor_tensor(out=o_sb[i][:, cols], in0=x_sb[b][o][:, tt, cols], scalar=coef[i][:, 1:2],
                                                in1=rdu.pop((i, n))[:], op0=ALU.mult, op1=ALU.add)
-            elif (i, n) in rdu:
-                nc.gpsimd.tensor_tensor(out=o_sb[i][:, cols], in0=rdu.pop((i, n))[:], in1=t_sb[i][:, cols], op=ALU.add)
             else:
-                nc.vector.scalar_tensor_tensor(out=o_sb[i][:, cols], in0=du[i, n][:], scalar=r_sb[:, o, b, tt : tt + 1],
-                                               in1=t_sb[i][:, cols], op0=ALU.mult, op1=ALU.add)
+                nc.vector.scalar_tensor_tensor(out=o_sb[i][:, cols], in0=x_sb[b][o][:, tt, cols], scalar=coef[i][:, 0:1],
+                                               in1=du[i, n][:], op0=ALU.mult, op1=ALU.add)
+
+        def add_g(i, n):
+            nc.gpsimd.tensor_tensor(out=o_sb[i][:, n * NT : (n + 1) * NT], in0=rdu.pop((i, n))[:], in1=t_sb.pop((i, n))[:], op=ALU.add)
+
+        def rescale(i, n0, n1, eng):
+            b, tt, o = where(i)
+            r = r_sb[:, o, b, tt : tt + 1]
+            if eng == "S":
+                nc.scalar.activation(out=o_sb[i][:, n0:n1], in_=o_sb[i][:, n0:n1], func=COPY, scale=r)
+            else:
+                nc.gpsimd.tensor_scalar(out=o_sb[i][:, n0:n1], in0=o_sb[i][:, n0:n1], scalar1=r, scalar2=0.0, op0=ALU.mult, op1=ALU.add)
 
         def store(i, n0, n1):
             b, tt, o = where(i)
@@ -219,8 +247,8 @@ def tile_interfusion_pa_v_kernel(tc, x1, x2, r1, r2, grad_0, grad_1, out_0, out_
 
             load_x(0, 0, 512)
             load_x(0, 512, 1024)
-            load_g(0)
             load_x(0, 1024, 2048)
+            load_g(0)
             load_x(1, 0, 1024)
             load_x(1, 1024, 2048)
             load_g(1)
@@ -228,6 +256,7 @@ def tile_interfusion_pa_v_kernel(tc, x1, x2, r1, r2, grad_0, grad_1, out_0, out_
             warm = keep.tile([P, 1], F32, name="warm")
             nc.vector.memset(warm[:], 0.0)
             nc.scalar.activation(out=warm[:], in_=warm[:], func=COPY)
+            nc.vector.tensor_scalar(out=nr1[:].rearrange("p i b j -> p (i b j)"), in0=r_sb[:].rearrange("p i b j -> p (i b j)"), scalar1=-1.0, scalar2=None, op0=ALU.mult)
             nc.vector.scalar_tensor_tensor(out=nr2[:].rearrange("p i b j -> p (i b j)"), in0=r_sb[:].rearrange("p i b j -> p (i b j)"),
                                            scalar=-1.0, in1=r_sb[:].rearrange("p i b j -> p (i b j)"), op0=ALU.mult, op1=ALU.mult)
 
@@ -236,16 +265,15 @@ def tile_interfusion_pa_v_kernel(tc, x1, x2, r1, r2, grad_0, grad_1, out_0, out_
                     u_scale(0, s)
                 if 1 <= s <= 8:
                     u_interleave(0, s - 1, (s - 1) in V_INTERLEAVE)
-                if s in (4, 5, 6):
-                    d_prepare(s - 4)
-                    d_round(s - 4)
-                if s == 6:
-                    d_quantize(0)
+                if s in D_AT:
+                    d_prepare(D_AT[s])
+                    d_round(D_AT[s])
+                if s in DQ_AT:
+                    d_quantize(DQ_AT[s])
                 if s == 8:
-                    d_quantize(1)
                     for m in range(3):
                         fill(m)
-                if s == 9:
+                if s == A_AT:
                     row_sum(0, 0)
                     row_sum(0, 1)
                 if s >= 2:
@@ -261,57 +289,67 @@ def tile_interfusion_pa_v_kernel(tc, x1, x2, r1, r2, grad_0, grad_1, out_0, out_
                 else:
                     u_scale_interleave(1, k)
 
-            for k in range(2):
+            for k in G_AT.get(-1, ()):
                 g_block(k)
 
-            quant_at = {1: (0,), 2: (1,), 3: (2,), 4: (3,), 5: (4,), 6: (5,), 7: (6, 7)}
             for i in range(16):
-                g_banks = G_BANKS.get(i, ())
+                share = G_BANKS.get(i, ())
+                mine = [n for n in range(NCH) if n not in share]
                 if i < 15:
                     row_sum(i, 2)
                     row_sum(i, 3)
-                    if 2 in g_banks:
-                        scaled_du(i, 2)
-                    coefficient(i)
-                    projection(i, 0)
-                    projection(i, 1)
-                    if 3 in g_banks:
-                        scaled_du(i, 3)
-                    for n in (2, 3) if 2 not in g_banks or 3 in g_banks else (3, 2):
+                    if share:
+                        scaled_du(i, share[0])
+                    coefficient(i, bool(share))
+                    for c, n in enumerate(share):
+                        if c > 0:
+                            scaled_du(i, n)
                         projection(i, n)
-                else:
-                    for n in g_banks:
-                        scaled_du(i, n)
-                    coefficient(i)
-                    projection(i, 0)
-                    projection(i, 1)
+                        add_g(i, n)
                 if i + 3 < 16:
                     d_round(i + 3)
-                for k in S_BLOCKS:
-                    if i == max(0, S_AT[k]):
+                for k in S_AT.get(i, ()):
+                    if k in S_BLOCKS:
                         u_interleave_s(1, k)
-                if i + 2 < 16 and i < 8:
+                if i + 2 < 16 and i in QD_EARLY:
                     d_quantize(i + 2)
-                for k in quant_at.get(i, ()):
+                for k in QUANT_AT.get(i, ()):
                     u_quantize(1, k)
-                    if k + 2 < 8:
-                        g_block(k + 2)
+                for k in G_AT.get(i, ()):
+                    g_block(k)
                 if i + 1 < 16:
                     row_sum(i + 1, 0)
                     row_sum(i + 1, 1)
-                if i + 2 < 16 and i >= 8:
-                    d_quantize(i + 2)
-                if i == 14:
-                    row_sum(15, 2)
-                    row_sum(15, 3)
-                for n in (2, 3, 0, 1) if i == 15 else range(NCH):
-                    finish(i, n)
+                for n in range(NCH):
+                    if n in mine or i == 15:
+                        project(i, n)
+                    if n == 0 and i + 2 < 16 and i not in QD_EARLY:
+                        d_quantize(i + 2)
+                    if n == 0 and i == 14:
+                        row_sum(15, 2)
+                        scaled_du(15, 2)
+                        row_sum(15, 3)
+                        scaled_du(15, 3)
+                        coefficient(15, True)
+                        if share and not STORE_LAST:
+                            store(i, len(mine) * NT, N)
                     if 4 * i + 6 + n < 62:
                         fill(4 * i + 6 + n)
                     if i == 15:
+                        if n < 2:
+                            rescale(i, n * NT, (n + 1) * NT, "S")
                         store(i, n * NT, (n + 1) * NT)
+                        if G_BANKS[14] and n == STORE_LAST - 1:
+                            store(14, N - len(G_BANKS[14]) * NT, N)
+                    elif share:
+                        if n == len(mine) - 1:
+                            rescale(i, 0, len(mine) * NT, R_ENG.get(i, "G"))
+                            store(i, 0, len(mine) * NT)
                     elif n % 2 == 1:
+                        rescale(i, (n - 1) * NT, (n + 1) * NT, "S")
                         store(i, (n - 1) * NT, (n + 1) * NT)
+                if share and i < 14:
+                    store(i, len(mine) * NT, N)
                 if i == 13:
                     fill(62)
                     fill(63)

from contextlib import ExitStack

import concourse.mybir as mybir
from concourse.masks import make_identity

F32 = mybir.dt.float32
BF16 = mybir.dt.bfloat16
U32 = mybir.dt.uint32
U8 = mybir.dt.uint8
E4X4 = mybir.dt.float8_e4m3fn_x4
E5X4 = mybir.dt.float8_e5m2_x4
ALU = mybir.AluOpType
COPY = mybir.ActivationFunctionType.Copy

NB, C, N = 2, 512, 2048
P = 128
J = 4
NT = 512
NCH = N // NT
FLOPS = 2 * 2 * NB * C * (2 * C) * N

V_INTERLEAVE = (0, 2, 4, 6)
GN = 128
G_BANKS = {8: (2, 3), 9: (2, 3), 10: (2, 3), 11: (2, 3), 12: (2, 3), 13: (3,), 14: (2, 3), 15: (2, 3), 1: (3,), 6: (3,), 7: (1, 2, 3), 3: (), 5: (), 2: (3,), 0: (), 4: ()}
R_ENG = {0: 'G', 1: 'S', 2: 'S', 3: 'S', 4: 'G', 5: 'S', 6: 'S', 7: 'G', 14: 'S', 9: 'G', 12: 'S', 8: 'G', 11: 'G', 10: 'S', 13: 'G'}
QD_EARLY = (0, 2, 3, 5, 6)
OB = 3
G1BUFS = 6
S_SCALE = (3,)
D_AT = {6: 0, 8: 1, 9: 2}
DQ_AT = {8: 0, 9: 1}
A_AT = 8
STORE_LAST = 0
S_PIECES = 1
S_BLOCKS = (1, 2, 3, 4, 5, 6, 7)
S_AT = {2: (0, 1), 4: (2, 3), 5: (4,), 6: (5, 6, 7)}
QUANT_AT = {2: (0,), 5: (1,), 6: (2, 3), 7: (4, 5, 6, 7)}
G_AT = {0: (0, 1, 2, 3), 4: (4,), 5: (5, 6, 7)}


def tile_interfusion_pa_v_kernel(tc, x1, x2, r1, r2, grad_0, grad_1, out_0, out_1):
    nc = tc.nc
    x_hbm = [x.rearrange("b (p j) h w -> b p j (h w)", j=J) for x in (x1, x2)]
    g_hbm = [g.rearrange("b (p j) w -> b p j w", j=J) for g in (grad_0, grad_1)]
    o_hbm = [o.rearrange("b (p j) h w -> b p j (h w)", j=J) for o in (out_0, out_1)]

    with ExitStack() as ctx:
        keep = ctx.enter_context(tc.tile_pool(name="keep", bufs=1))
        stage = ctx.enter_context(tc.tile_pool(name="stage", bufs=3))
        psum_du = ctx.enter_context(tc.psum_pool(name="psum_du", bufs=6))
        psum_d = ctx.enter_context(tc.psum_pool(name="psum_d", bufs=2))

        ident = keep.tile([P, P], BF16, name="ident", align_bytes=64)
        make_identity(nc, ident[:])
        r_sb = keep.tile([P, 2, NB, J], F32, name="r_sb")
        r_late = keep.tile([P, 2, J], F32, name="r_late")
        nr1 = keep.tile([P, 2, NB, J], F32, name="nr1")
        nr2 = keep.tile([P, 2, NB, J], F32, name="nr2")
        x_sb = [[keep.tile([P, J, N], BF16, name="x_%d_%d" % (b, i), align_bytes=64) for i in range(2)] for b in range(NB)]
        g_sb = [[keep.tile([P, J, C], BF16, name="g_%d_%d" % (b, i), align_bytes=64) for i in range(2)] for b in range(NB)]
        u_codes = [keep.tile([P, 2, N], U32, name="uc_%d" % b, align_bytes=64) for b in range(NB)]
        u_scales = [keep.tile([P, 2, N], U8, name="us_%d" % b, align_bytes=64) for b in range(NB)]

        scaled = {}
        grouped = {}
        d_banks = {}
        d_grouped = {}
        d_codes = {}
        d_scales = {}
        du = {}
        q4 = {}
        coef = {}
        t_sb = {}
        rdu = {}
        o_sb = {}

        def where(i):
            return i // 8, i % 4, 1 if i % 8 < 4 else 0

        def u_scale(b, k):
            n, xi = k // 2, k % 2
            s = stage.tile([P, J, NT], BF16, name="scaled", bufs=3, align_bytes=64)
            for j in range(J):
                src = x_sb[b][xi][:, j, n * NT : (n + 1) * NT]
                r = r_sb[:, xi, b, j : j + 1]
                if k in S_SCALE:
                    nc.scalar.activation(out=s[:, j, :], in_=src, func=COPY, scale=r)
                else:
                    nc.vector.tensor_scalar(out=s[:, j, :], in0=src, scalar1=r, scalar2=None, op0=ALU.mult)
            scaled[b, k] = s

        def u_interleave(b, k, on_vector):
            g = stage.tile([P, NT, J], BF16, name="grouped", bufs=3, align_bytes=64)
            src = scaled.pop((b, k))[:].rearrange("p j (c i) -> p c j i", i=4)
            dst = g[:].rearrange("p (c i) j -> p c j i", i=4)
            if on_vector:
                nc.vector.tensor_copy(out=dst, in_=src)
            else:
                nc.scalar.copy(out=dst, in_=src)
            grouped[b, k] = g

        def u_scale_interleave(b, k):
            n, xi = k // 2, k % 2
            g = stage.tile([P, NT, J], BF16, name="grouped1", bufs=G1BUFS, align_bytes=64)
            for c in range(0, NT, GN):
                nc.gpsimd.tensor_tensor(out=g[:, c : c + GN, :], in0=x_sb[b][xi][:, :, n * NT + c : n * NT + c + GN].rearrange("p j n -> p n j"),
                                        in1=r_late[:, xi, :].unsqueeze(1).to_broadcast([P, GN, J]), op=ALU.mult)
            grouped[b, k] = g

        def u_scale_g(b, k):
            n, xi = k // 2, k % 2
            s = stage.tile([P, 2, NT, 2], BF16, name="scaled", bufs=3, align_bytes=64)
            for j in range(J):
                nc.gpsimd.tensor_scalar(out=s[:, j // 2, :, j % 2], in0=x_sb[b][xi][:, j, n * NT : (n + 1) * NT],
                                        scalar1=r_late[:, xi, j : j + 1], scalar2=0.0, op0=ALU.mult, op1=ALU.add)
            scaled[b, k] = s

        def u_interleave_s(b, k):
            g = stage.tile([P, NT, J], BF16, name="grouped1", bufs=G1BUFS, align_bytes=64)
            s = scaled.pop((b, k))[:].rearrange("p u n e -> p u (n e)").bitcast(F32)
            d = g[:].bitcast(F32)
            for c in range(0, NT, NT // S_PIECES):
                nc.scalar.copy(out=d[:, c : c + NT // S_PIECES, :], in_=s[:, :, c : c + NT // S_PIECES].rearrange("p u n -> p n u"))
            grouped[b, k] = g

        def u_quantize(b, k):
            n, xi = k // 2, k % 2
            cols = slice(n * NT, (n + 1) * NT)
            nc.vector.quantize_mx(out=u_codes[b][:, xi, cols].bitcast(E4X4), scales=u_scales[b][:, xi, cols],
                                  in_=grouped.pop((b, k))[:].rearrange("p n j -> p (n j)"))

        def d_prepare(i):
            b, tt, o = where(i)
            banks = []
            for ps in range(2):
                if o == 0 and ps == 1:
                    bank = psum_d.tile([P, J, P], BF16, name="dbank")
                    for t in range(J):
                        nc.tensor.transpose(bank[:, t, :], d_grouped[8 * b + t][:, 0, :, tt], ident[:])
                else:
                    bank = psum_d.tile([P, J, P], F32, name="dbank")
                    for t in range(J):
                        nc.tensor.matmul(bank[:, t, :], lhsT=ident[:], rhs=g_sb[b][o][:, t, tt::J], start=True, stop=False)
                        nc.tensor.matmul(bank[:, t, :], lhsT=g_sb[b][ps][:, tt, t::J], rhs=ident[:], start=False, stop=True)
                banks.append(bank)
            d_banks[i] = banks

        def d_round(i):
            if where(i)[2] == 1:
                dg = stage.tile([P, 2, P, J], BF16, name="dg1", bufs=4, align_bytes=64)
            else:
                dg = stage.tile([P, 2, P, J], BF16, name="dg0", bufs=3, align_bytes=64)
            for ps in range(2):
                nc.scalar.copy(out=dg[:, ps, :, :], in_=d_banks[i][ps][:].rearrange("p t m -> p m t"))
            d_grouped[i] = dg

        def d_quantize(i):
            dc = stage.tile([P, 2 * P], U32, name="dc", bufs=6, align_bytes=64)
            dsc = stage.tile([P, 2 * P], U8, name="dsc", bufs=6, align_bytes=64)
            nc.vector.quantize_mx(out=dc[:].bitcast(E5X4), scales=dsc[:], in_=d_grouped[i][:].rearrange("p s m t -> p (s m t)"))
            d_codes[i], d_scales[i] = dc, dsc

        def fill(m):
            i, n = m // NCH, m % NCH
            b = where(i)[0]
            if m < 62:
                bank = psum_du.tile([P, NT], F32, name="du")
            else:
                bank = psum_d.tile([P, NT], F32, name="dbank")
            cols = slice(n * NT, (n + 1) * NT)
            for ps in range(2):
                ks = slice(ps * P, (ps + 1) * P)
                nc.tensor.matmul_mx(out=bank[:], lhsT=d_codes[i][:, ks].bitcast(E5X4), lhsT_scale=d_scales[i][:, ks],
                                    rhs=u_codes[b][:, ps, cols].bitcast(E4X4), rhs_scale=u_scales[b][:, ps, cols],
                                    start=(ps == 0), stop=(ps == 1))
            du[i, n] = bank

        def row_sum(i, n):
            b, tt, o = where(i)
            if n == 0:
                q = stage.tile([P, NCH], F32, name="q4", bufs=3)
                q4[i] = q
            junk = stage.tile([P, NT], BF16, name="junk", bufs=4)
            nc.vector.scalar_tensor_tensor(out=junk[:], in0=du[i, n][:], scalar=r_sb[:, o, b, tt : tt + 1],
                                           in1=x_sb[b][o][:, tt, n * NT : (n + 1) * NT], op0=ALU.mult, op1=ALU.mult,
                                           accum_out=q4[i][:, n : n + 1])

        def coefficient(i, both):
            b, tt, o = where(i)
            cf = stage.tile([P, 2], F32, name="cf", bufs=3)
            junk4 = stage.tile([P, 2, NCH], F32, name="junk4", bufs=3)
            for v in range(2 if both else 1):
                nc.scalar.activation(out=junk4[:, v, :], in_=q4[i][:], func=COPY, scale=(nr1, nr2)[v][:, o, b, tt : tt + 1],
                                     accum_out=cf[:, v : v + 1])
            coef[i] = cf
            ob = stage.tile([P, N], F32, name="o", bufs=OB)
            o_sb[i] = ob

        def projection(i, n):
            b, tt, o = where(i)
            t = stage.tile([P, NT], F32, name="t", bufs=4)
            nc.scalar.activation(out=t[:], in_=x_sb[b][o][:, tt, n * NT : (n + 1) * NT], func=COPY, scale=coef[i][:, 1:2])
            t_sb[i, n] = t

        def scaled_du(i, n):
            b, tt, o = where(i)
            rd = stage.tile([P, NT], F32, name="rdu", bufs=4)
            nc.scalar.activation(out=rd[:], in_=du[i, n][:], func=COPY, scale=r_sb[:, o, b, tt : tt + 1])
            rdu[i, n] = rd

        def project(i, n):
            b, tt, o = where(i)
            cols = slice(n * NT, (n + 1) * NT)
            if (i, n) in rdu:
                nc.vector.scalar_tensor_tensor(out=o_sb[i][:, cols], in0=x_sb[b][o][:, tt, cols], scalar=coef[i][:, 1:2],
                                               in1=rdu.pop((i, n))[:], op0=ALU.mult, op1=ALU.add)
            else:
                nc.vector.scalar_tensor_tensor(out=o_sb[i][:, cols], in0=x_sb[b][o][:, tt, cols], scalar=coef[i][:, 0:1],
                                               in1=du[i, n][:], op0=ALU.mult, op1=ALU.add)

        def add_g(i, n):
            nc.gpsimd.tensor_tensor(out=o_sb[i][:, n * NT : (n + 1) * NT], in0=rdu.pop((i, n))[:], in1=t_sb.pop((i, n))[:], op=ALU.add)

        def rescale(i, n0, n1, eng):
            b, tt, o = where(i)
            r = r_sb[:, o, b, tt : tt + 1]
            if eng == "S":
                nc.scalar.activation(out=o_sb[i][:, n0:n1], in_=o_sb[i][:, n0:n1], func=COPY, scale=r)
            else:
                nc.gpsimd.tensor_scalar(out=o_sb[i][:, n0:n1], in0=o_sb[i][:, n0:n1], scalar1=r, scalar2=0.0, op0=ALU.mult, op1=ALU.add)

        def store(i, n0, n1):
            b, tt, o = where(i)
            nc.sync.dma_start(out=o_hbm[o][b, :, tt, n0:n1], in_=o_sb[i][:, n0:n1])

        with tc.manual_schedule():
            for xi, r in enumerate((r1, r2)):
                nc.scalar.dma_start(out=r_sb[:, xi, :, :], in_=r.rearrange("b (p j) -> p b j", j=J))

            def load_x(b, n0, n1):
                for xi in range(2):
                    nc.sync.dma_start(out=x_sb[b][xi][:, :, n0:n1], in_=x_hbm[xi][b, :, :, n0:n1])

            def load_g(b):
                for gi in range(2):
                    nc.sync.dma_start(out=g_sb[b][gi][:], in_=g_hbm[gi][b])

            load_x(0, 0, 512)
            load_x(0, 512, 1024)
            load_x(0, 1024, 2048)
            load_g(0)
            load_x(1, 0, 1024)
            load_x(1, 1024, 2048)
            load_g(1)

            warm = keep.tile([P, 1], F32, name="warm")
            nc.vector.memset(warm[:], 0.0)
            nc.scalar.activation(out=warm[:], in_=warm[:], func=COPY)
            nc.vector.tensor_scalar(out=nr1[:].rearrange("p i b j -> p (i b j)"), in0=r_sb[:].rearrange("p i b j -> p (i b j)"), scalar1=-1.0, scalar2=None, op0=ALU.mult)
            nc.vector.scalar_tensor_tensor(out=nr2[:].rearrange("p i b j -> p (i b j)"), in0=r_sb[:].rearrange("p i b j -> p (i b j)"),
                                           scalar=-1.0, in1=r_sb[:].rearrange("p i b j -> p (i b j)"), op0=ALU.mult, op1=ALU.mult)

            for s in range(10):
                if s < 8:
                    u_scale(0, s)
                if 1 <= s <= 8:
                    u_interleave(0, s - 1, (s - 1) in V_INTERLEAVE)
                if s in D_AT:
                    d_prepare(D_AT[s])
                    d_round(D_AT[s])
                if s in DQ_AT:
                    d_quantize(DQ_AT[s])
                if s == 8:
                    for m in range(3):
                        fill(m)
                if s == A_AT:
                    row_sum(0, 0)
                    row_sum(0, 1)
                if s >= 2:
                    u_quantize(0, s - 2)
            nc.vector.tensor_copy(out=r_late[:], in_=r_sb[:, :, 1, :])
            fill(3)
            fill(4)
            fill(5)
            d_prepare(3)
            def g_block(k):
                if k in S_BLOCKS:
                    u_scale_g(1, k)
                else:
                    u_scale_interleave(1, k)

            for k in G_AT.get(-1, ()):
                g_block(k)

            for i in range(16):
                share = G_BANKS.get(i, ())
                mine = [n for n in range(NCH) if n not in share]
                if i < 15:
                    row_sum(i, 2)
                    row_sum(i, 3)
                    if share:
                        scaled_du(i, share[0])
                    coefficient(i, bool(share))
                    for c, n in enumerate(share):
                        if c > 0:
                            scaled_du(i, n)
                        projection(i, n)
                        add_g(i, n)
                if i + 3 < 16:
                    d_round(i + 3)
                for k in S_AT.get(i, ()):
                    if k in S_BLOCKS:
                        u_interleave_s(1, k)
                if i + 2 < 16 and i in QD_EARLY:
                    d_quantize(i + 2)
                for k in QUANT_AT.get(i, ()):
                    u_quantize(1, k)
                for k in G_AT.get(i, ()):
                    g_block(k)
                if i + 1 < 16:
                    row_sum(i + 1, 0)
                    row_sum(i + 1, 1)
                for n in range(NCH):
                    if n in mine or i == 15:
                        project(i, n)
                    if n == 0 and i + 2 < 16 and i not in QD_EARLY:
                        d_quantize(i + 2)
                    if n == 0 and i == 14:
                        row_sum(15, 2)
                        scaled_du(15, 2)
                        row_sum(15, 3)
                        scaled_du(15, 3)
                        coefficient(15, True)
                        if share and not STORE_LAST:
                            store(i, len(mine) * NT, N)
                    if 4 * i + 6 + n < 62:
                        fill(4 * i + 6 + n)
                    if i == 15:
                        if n < 2:
                            rescale(i, n * NT, (n + 1) * NT, "S")
                        store(i, n * NT, (n + 1) * NT)
                        if G_BANKS[14] and n == STORE_LAST - 1:
                            store(14, N - len(G_BANKS[14]) * NT, N)
                    elif share:
                        if n == len(mine) - 1:
                            rescale(i, 0, len(mine) * NT, R_ENG.get(i, "G"))
                            store(i, 0, len(mine) * NT)
                    elif n % 2 == 1:
                        rescale(i, (n - 1) * NT, (n + 1) * NT, "S")
                        store(i, (n - 1) * NT, (n + 1) * NT)
                if share and i < 14:
                    store(i, len(mine) * NT, N)
                if i == 13:
                    fill(62)
                    fill(63)
                if i + 4 < 16:
                    d_prepare(i + 4)
